import numpy as np
import ml_dtypes


def mxq(x, axis, fmt="e4m3"):
    dtype, down = {"e4m3": (ml_dtypes.float8_e4m3fn, 7), "e5m2": (ml_dtypes.float8_e5m2, 14)}[fmt]
    v = np.moveaxis(np.asarray(x, np.float32).astype(ml_dtypes.bfloat16).astype(np.float64), axis, -1)
    blocks = v.reshape(v.shape[:-1] + (-1, 32))
    amax = np.abs(blocks).max(-1, keepdims=True)
    byte = np.maximum(np.where(amax > 0, np.frexp(amax)[1] - 1 + 127, 0) - down, 1)
    scale = np.exp2(byte - 127.0)
    codes = (blocks / scale).astype(np.float32).astype(dtype).astype(np.float64)
    return np.moveaxis((codes * scale).reshape(v.shape), -1, axis)


WIDE = False


def mx_kscale(k):
    if not WIDE:
        return np.ones(k)
    levels = np.array([10, -10, 5, -5, 0])
    a = np.random.permutation(np.resize(levels, k // 512 * 4)).reshape(k // 512, 4)
    idx = np.arange(k)
    return np.exp2(a[idx // 512, idx % 128 // 32])


BF16 = ml_dtypes.bfloat16


def bf(x):
    return np.asarray(x, np.float32).astype(BF16)


def f64(x):
    return np.asarray(x).astype(np.float64)


B, Q, K, D = 2, 128, 512, 512
NEG = -10000.0


def setup_inputs():
    s, t = mx_kscale(D), mx_kscale(D)
    return {"query": bf(np.random.standard_normal((B, Q, D)) * s),
            "context": bf(np.random.standard_normal((B, K, D)) * 0.5 / t),
            "query_bit": bf(np.random.random((B, Q)) > 0.25),
            "context_bit": bf(np.random.random((B, K)) > 0.25),
            "W_in": bf(np.random.standard_normal((D, D)) * 4.0 / D * t[:, None] / s[None, :]),
            "b_in": bf(np.random.standard_normal(D) / np.sqrt(D) * t)}


def reference(query, context, query_bit, context_bit, W_in, b_in):
    ext = (1.0 - f64(query_bit)[:, :, None] * f64(context_bit)[:, None, :]) * NEG
    q = (mxq(f64(query), 2, "e4m3") @ mxq(f64(W_in), 1, "e4m3").T) + f64(b_in)
    scores = (mxq(q, 2, "e4m3") @ mxq(f64(context), 2, "e4m3").transpose(0, 2, 1)) + ext
    e = np.exp(scores - scores.max(-1, keepdims=True))
    return e / e.sum(-1, keepdims=True)

@@ -1,0 +1,200 @@
+from contextlib import ExitStack
+
+import concourse.mybir as mybir
+from concourse.masks import make_identity
+
+F32 = mybir.dt.float32
+BF16 = mybir.dt.bfloat16
+U32 = mybir.dt.uint32
+U8 = mybir.dt.uint8
+FP8X4 = mybir.dt.float8_e4m3fn_x4
+ALU = mybir.AluOpType
+ACT = mybir.ActivationFunctionType
+
+P = 128
+B = 2
+Q = 128
+K = 512
+D = 512
+PACK = 4
+NEG = -10000.0
+
+FLOPS = 2 * B * Q * D * D + 2 * B * Q * K * D
+
+
+def transpose_two_row_tiles(nc, psum, words, ident):
+    bank = psum.tile([P, 2, 2, P], F32)
+    for a in range(2):
+        for u in range(2):
+            nc.tensor.transpose(bank[:, a, u, :], words[:, a, u * P : (u + 1) * P], ident[:])
+    return bank
+
+
+def regrouped(bank):
+    return bank[:].rearrange("p a u r -> p a r u")
+
+
+def tile_attention_pa_s_kernel(tc, query, context, query_bit, context_bit, W_in, b_in, out):
+    nc = tc.nc
+    with ExitStack() as ctx:
+        keep = ctx.enter_context(tc.tile_pool(name="keep", bufs=1))
+        tp = ctx.enter_context(tc.psum_pool(name="tp", bufs=4))
+        spread = ctx.enter_context(tc.psum_pool(name="spread", bufs=1))
+        acc = ctx.enter_context(tc.psum_pool(name="acc", bufs=2))
+
+        cb_col = keep.tile([P, B, 4], BF16)
+        qb_col = keep.tile([P, B], BF16)
+        bias_col = keep.tile([P, 2, 2], BF16)
+        nc.scalar.dma_start(out=cb_col[:], in_=context_bit.rearrange("b (p c) -> p b c", c=4))
+        with nc.allow_non_contiguous_dma(reason="256 single elements, one to a partition and batch"):
+            nc.scalar.dma_start(out=qb_col[:], in_=query_bit.rearrange("b i -> i b"))
+        nc.scalar.dma_start(out=bias_col[:], in_=b_in.rearrange("(u p e) -> p u e", u=2, e=2))
+
+        query_sb = keep.tile([P, B, D], BF16)
+        w_sb = keep.tile([P, 2, 2, D], BF16)
+        ctx_sb = keep.tile([P, B, 4, D], BF16)
+        nc.sync.dma_start(out=query_sb[:], in_=query.rearrange("b i d -> i b d"))
+        w_rows = W_in.rearrange("(u p e) d -> u p e d", u=2, e=2)
+        for u in range(2):
+            nc.sync.dma_start(out=w_sb[:, u], in_=w_rows[u])
+        for b in range(B):
+            ctx_rows = context[b].rearrange("(p c) d -> p c d", c=4)
+            for h in range(2):
+                nc.sync.dma_start(out=ctx_sb[:, b, 2 * h : 2 * h + 2], in_=ctx_rows[:, 2 * h : 2 * h + 2, :])
+
+        ident_f32 = keep.tile([P, P], F32)
+        make_identity(nc, ident_f32[:])
+        ident_bf16 = keep.tile([P, P], BF16)
+        make_identity(nc, ident_bf16[:])
+        warm = keep.tile([P, 1], F32)
+        nc.vector.memset(warm[:], 0.0)
+        nc.scalar.activation(out=warm[:], in_=warm[:], func=ACT.Exp)
+
+        not_cb = keep.tile([P, B, 4], BF16)
+        nc.gpsimd.tensor_scalar(out=not_cb[:], in0=cb_col[:], scalar1=-1.0, scalar2=1.0, op0=ALU.mult, op1=ALU.add)
+        neg_qb = keep.tile([P, B], F32)
+        nc.gpsimd.tensor_scalar(out=neg_qb[:], in0=qb_col[:], scalar1=NEG, scalar2=0.0, op0=ALU.mult, op1=ALU.add)
+        bias_f32 = keep.tile([P, PACK], F32)
+        nc.gpsimd.tensor_copy(out=bias_f32[:], in_=bias_col[:].rearrange("p u e -> p (u e)"))
+
+        query_grp = keep.tile([P, B, Q, PACK], BF16, align_bytes=64)
+        query_codes = keep.tile([P, B, Q], U32, align_bytes=64)
+        query_scales = keep.tile([P, B, Q], U8, align_bytes=64)
+        w_grp = keep.tile([P, 2, 2, P, PACK], BF16, align_bytes=64)
+        w_codes = keep.tile([P, 2, 2, P], U32, align_bytes=64)
+        w_scales = keep.tile([P, 2, 2, P], U8, align_bytes=64)
+        ctx_grp = keep.tile([P, B, 2, 2, P, PACK], BF16, align_bytes=64)
+        ctx_codes = keep.tile([P, B, 2, 2, P], U32, align_bytes=64)
+        ctx_scales = keep.tile([P, B, 2, 2, P], U8, align_bytes=64)
+        qt_grp = keep.tile([P, B, Q, PACK], BF16, align_bytes=64)
+        qt_codes = keep.tile([P, B, Q], U32, align_bytes=64)
+        qt_scales = keep.tile([P, B, Q], U8, align_bytes=64)
+
+        bank = transpose_two_row_tiles(nc, tp, query_sb[:].bitcast(F32), ident_f32)
+        nc.vector.tensor_copy(out=query_grp[:].bitcast(F32), in_=regrouped(bank))
+        nc.vector.quantize_mx(
+            out=query_codes[:].rearrange("p b i -> p (b i)").bitcast(FP8X4),
+            scales=query_scales[:].rearrange("p b i -> p (b i)"),
+            in_=query_grp[:].rearrange("p b i t -> p (b i t)"),
+        )
+        for u in range(2):
+            bank = transpose_two_row_tiles(nc, tp, w_sb[:].bitcast(F32)[:, u], ident_f32)
+            nc.scalar.copy(out=w_grp[:, u].bitcast(F32), in_=regrouped(bank))
+            nc.vector.quantize_mx(
+                out=w_codes[:, u].rearrange("p e m -> p (e m)").bitcast(FP8X4),
+                scales=w_scales[:, u].rearrange("p e m -> p (e m)"),
+                in_=w_grp[:, u].rearrange("p e m t -> p (e m t)"),
+            )
+
+        spread_ps = spread.tile([P, B, 4, P], BF16)
+        for b in range(B):
+            for c in range(4):
+                nc.tensor.transpose(spread_ps[:, b, c, :], not_cb[:, b, c : c + 1].to_broadcast([P, P]), ident_bf16[:])
+        not_cb_all = keep.tile([P, B, K], BF16)
+        nc.vector.tensor_copy(out=not_cb_all[:], in_=spread_ps[:].rearrange("p b c n -> p b (c n)"))
+
+        def context_chunk(b, h):
+            bank = transpose_two_row_tiles(nc, tp, ctx_sb[:].bitcast(F32)[:, b, 2 * h : 2 * h + 2], ident_f32)
+            nc.scalar.copy(out=ctx_grp[:, b, h].bitcast(F32), in_=regrouped(bank))
+            nc.vector.quantize_mx(
+                out=ctx_codes[:, b, h].rearrange("p a n -> p (a n)").bitcast(FP8X4),
+                scales=ctx_scales[:, b, h].rearrange("p a n -> p (a n)"),
+                in_=ctx_grp[:, b, h].rearrange("p a n t -> p (a n t)"),
+            )
+
+        context_chunk(0, 0)
+        context_chunk(0, 1)
+
+        for b in range(B):
+            qt_ps = acc.tile([P, PACK, Q], F32, tag="acc")
+            for u in range(2):
+                for e in range(2):
+                    nc.tensor.matmul_mx(
+                        out=qt_ps[:, 2 * u + e, :],
+                        lhsT=w_codes[:, u, e, :].bitcast(FP8X4),
+                        lhsT_scale=w_scales[:, u, e, :],
+                        rhs=query_codes[:, b, :].bitcast(FP8X4),
+                        rhs_scale=query_scales[:, b, :],
+                        start=True,
+                        stop=True,
+                    )
+            nc.vector.tensor_tensor(
+                out=qt_grp[:, b],
+                in0=qt_ps[:].rearrange("p t i -> p i t"),
+                in1=bias_f32[:].unsqueeze(1).to_broadcast([P, Q, PACK]),
+                op=ALU.add,
+            )
+            nc.vector.quantize_mx(
+                out=qt_codes[:, b, :].bitcast(FP8X4),
+                scales=qt_scales[:, b, :],
+                in_=qt_grp[:, b].rearrange("p i t -> p (i t)"),
+            )
+
+        context_chunk(1, 0)
+        context_chunk(1, 1)
+
+        masked = keep.tile([P, B, K], F32)
+        expd = keep.tile([P, B, K], F32)
+        prob = keep.tile([P, B, K], F32)
+        neg_max = keep.tile([P, B], F32)
+        row_sum = keep.tile([P, B], F32)
+        inv_sum = keep.tile([P, B], F32)
+        for b in range(B):
+            score_ps = acc.tile([P, K], F32, tag="acc")
+            nc.tensor.matmul_mx(
+                out=score_ps[:],
+                lhsT=qt_codes[:, b, :].bitcast(FP8X4),
+                lhsT_scale=qt_scales[:, b, :],
+                rhs=ctx_codes[:, b].rearrange("p h a n -> p (h a n)").bitcast(FP8X4),
+                rhs_scale=ctx_scales[:, b].rearrange("p h a n -> p (h a n)"),
+                start=True,
+                stop=True,
+            )
+            nc.vector.scalar_tensor_tensor(
+                out=masked[:, b, :],
+                in0=not_cb_all[:, b, :],
+                scalar=neg_qb[:, b : b + 1],
+                in1=score_ps[:],
+                op0=ALU.mult,
+                op1=ALU.add,
+            )
+            nc.vector.tensor_reduce(
+                out=neg_max[:, b : b + 1], in_=masked[:, b, :], axis=mybir.AxisListType.X, op=ALU.max, negate=True
+            )
+            nc.scalar.activation(
+                out=expd[:, b, :],
+                in_=masked[:, b, :],
+                func=ACT.Exp,
+                bias=neg_max[:, b : b + 1],
+                scale=1.0,
+                accum_out=row_sum[:, b : b + 1],
+            )
+            nc.vector.reciprocal(inv_sum[:, b : b + 1], row_sum[:, b : b + 1])
+            nc.vector.tensor_scalar(
+                out=prob[:, b, :].rearrange("i (p c) -> i p c", c=4),
+                in0=expd[:, b, :].rearrange("i (c p) -> i p c", c=4),
+                scalar1=inv_sum[:, b : b + 1],
+                scalar2=None,
+                op0=ALU.mult,
+            )
+            nc.sync.dma_start(out=out[b], in_=prob[:, b, :])

@@ -22,18 +22,6 @@ NEG = -10000.0
 FLOPS = 2 * B * Q * D * D + 2 * B * Q * K * D
 
 
-def transpose_two_row_tiles(nc, psum, words, ident):
-    bank = psum.tile([P, 2, 2, P], F32)
-    for a in range(2):
-        for u in range(2):
-            nc.tensor.transpose(bank[:, a, u, :], words[:, a, u * P : (u + 1) * P], ident[:])
-    return bank
-
-
-def regrouped(bank):
-    return bank[:].rearrange("p a u r -> p a r u")
-
-
 def tile_attention_pa_s_kernel(tc, query, context, query_bit, context_bit, W_in, b_in, out):
     nc = tc.nc
     with ExitStack() as ctx:
@@ -41,41 +29,38 @@ def tile_attention_pa_s_kernel(tc, query, context, query_bit, context_bit, W_in,
         tp = ctx.enter_context(tc.psum_pool(name="tp", bufs=4))
         spread = ctx.enter_context(tc.psum_pool(name="spread", bufs=1))
         acc = ctx.enter_context(tc.psum_pool(name="acc", bufs=2))
-
-        cb_col = keep.tile([P, B, 4], BF16)
-        qb_col = keep.tile([P, B], BF16)
-        bias_col = keep.tile([P, 2, 2], BF16)
-        nc.scalar.dma_start(out=cb_col[:], in_=context_bit.rearrange("b (p c) -> p b c", c=4))
-        with nc.allow_non_contiguous_dma(reason="256 single elements, one to a partition and batch"):
-            nc.scalar.dma_start(out=qb_col[:], in_=query_bit.rearrange("b i -> i b"))
-        nc.scalar.dma_start(out=bias_col[:], in_=b_in.rearrange("(u p e) -> p u e", u=2, e=2))
+        ctx.enter_context(tc.manual_schedule())
 
         query_sb = keep.tile([P, B, D], BF16)
         w_sb = keep.tile([P, 2, 2, D], BF16)
-        ctx_sb = keep.tile([P, B, 4, D], BF16)
-        nc.sync.dma_start(out=query_sb[:], in_=query.rearrange("b i d -> i b d"))
+        ctx_sb = keep.tile([P, B, 2, 2, D], BF16)
+        cb_col = keep.tile([P, B, 2, 2], BF16)
+        qb_col = keep.tile([P, B], BF16)
+        bias_col = keep.tile([P, PACK], BF16)
         w_rows = W_in.rearrange("(u p e) d -> u p e d", u=2, e=2)
+        ctx_rows = context.rearrange("b (p g e) d -> b g p e d", g=2, e=2)
+        for b in range(B):
+            nc.sync.dma_start(out=query_sb[:, b, :], in_=query[b])
         for u in range(2):
             nc.sync.dma_start(out=w_sb[:, u], in_=w_rows[u])
-        for b in range(B):
-            ctx_rows = context[b].rearrange("(p c) d -> p c d", c=4)
-            for h in range(2):
-                nc.sync.dma_start(out=ctx_sb[:, b, 2 * h : 2 * h + 2], in_=ctx_rows[:, 2 * h : 2 * h + 2, :])
+        nc.sync.dma_start(out=ctx_sb[:, 0, 0], in_=ctx_rows[0, 0])
+        nc.sync.dma_start(
+            out=bias_col[:].rearrange("p (u e) -> p u e", u=2), in_=b_in.rearrange("(u p e) -> p u e", u=2, e=2)
+        )
+        nc.sync.dma_start(out=ctx_sb[:, 0, 1], in_=ctx_rows[0, 1])
+        nc.sync.dma_start(
+            out=cb_col[:].rearrange("p b g e -> p b (g e)"), in_=context_bit.rearrange("b (p c) -> p b c", c=4)
+        )
+        with nc.allow_non_contiguous_dma(reason="256 single elements, one to a partition and batch"):
+            nc.sync.dma_start(out=qb_col[:], in_=query_bit.rearrange("b i -> i b"))
+        nc.sync.dma_start(out=ctx_sb[:, 1, 0], in_=ctx_rows[1, 0])
+        nc.sync.dma_start(out=ctx_sb[:, 1, 1], in_=ctx_rows[1, 1])
 
-        ident_f32 = keep.tile([P, P], F32)
-        make_identity(nc, ident_f32[:])
-        ident_bf16 = keep.tile([P, P], BF16)
-        make_identity(nc, ident_bf16[:])
+        ident = keep.tile([P, P], F32)
+        make_identity(nc, ident[:])
         warm = keep.tile([P, 1], F32)
         nc.vector.memset(warm[:], 0.0)
         nc.scalar.activation(out=warm[:], in_=warm[:], func=ACT.Exp)
-
-        not_cb = keep.tile([P, B, 4], BF16)
-        nc.gpsimd.tensor_scalar(out=not_cb[:], in0=cb_col[:], scalar1=-1.0, scalar2=1.0, op0=ALU.mult, op1=ALU.add)
-        neg_qb = keep.tile([P, B], F32)
-        nc.gpsimd.tensor_scalar(out=neg_qb[:], in0=qb_col[:], scalar1=NEG, scalar2=0.0, op0=ALU.mult, op1=ALU.add)
-        bias_f32 = keep.tile([P, PACK], F32)
-        nc.gpsimd.tensor_copy(out=bias_f32[:], in_=bias_col[:].rearrange("p u e -> p (u e)"))
 
         query_grp = keep.tile([P, B, Q, PACK], BF16, align_bytes=64)
         query_codes = keep.tile([P, B, Q], U32, align_bytes=64)
@@ -83,49 +68,52 @@ def tile_attention_pa_s_kernel(tc, query, context, query_bit, context_bit, W_in,
         w_grp = keep.tile([P, 2, 2, P, PACK], BF16, align_bytes=64)
         w_codes = keep.tile([P, 2, 2, P], U32, align_bytes=64)
         w_scales = keep.tile([P, 2, 2, P], U8, align_bytes=64)
-        ctx_grp = keep.tile([P, B, 2, 2, P, PACK], BF16, align_bytes=64)
-        ctx_codes = keep.tile([P, B, 2, 2, P], U32, align_bytes=64)
-        ctx_scales = keep.tile([P, B, 2, 2, P], U8, align_bytes=64)
+        ctx_grp = keep.tile([P, B, 2, P, 2, PACK], BF16, align_bytes=64)
+        ctx_codes = keep.tile([P, B, 2, 2 * P], U32, align_bytes=64)
+        ctx_scales = keep.tile([P, B, 2, 2 * P], U8, align_bytes=64)
         qt_grp = keep.tile([P, B, Q, PACK], BF16, align_bytes=64)
         qt_codes = keep.tile([P, B, Q], U32, align_bytes=64)
         qt_scales = keep.tile([P, B, Q], U8, align_bytes=64)
 
-        bank = transpose_two_row_tiles(nc, tp, query_sb[:].bitcast(F32), ident_f32)
-        nc.vector.tensor_copy(out=query_grp[:].bitcast(F32), in_=regrouped(bank))
-        nc.vector.quantize_mx(
-            out=query_codes[:].rearrange("p b i -> p (b i)").bitcast(FP8X4),
-            scales=query_scales[:].rearrange("p b i -> p (b i)"),
-            in_=query_grp[:].rearrange("p b i t -> p (b i t)"),
-        )
-        for u in range(2):
-            bank = transpose_two_row_tiles(nc, tp, w_sb[:].bitcast(F32)[:, u], ident_f32)
-            nc.scalar.copy(out=w_grp[:, u].bitcast(F32), in_=regrouped(bank))
-            nc.vector.quantize_mx(
-                out=w_codes[:, u].rearrange("p e m -> p (e m)").bitcast(FP8X4),
-                scales=w_scales[:, u].rearrange("p e m -> p (e m)"),
-                in_=w_grp[:, u].rearrange("p e m t -> p (e m t)"),
+        def transpose_two_row_tiles(words):
+            bank = tp.tile([P, 2, 2, P], F32)
+            for a in range(2):
+                for u in range(2):
+                    nc.tensor.transpose(bank[:, a, u, :], words[:, a, u * P : (u + 1) * P], ident[:])
+            return bank
+
+        def quantise(grp, codes, scales):
+            nc.vector.quantize_mx(out=codes.bitcast(FP8X4), scales=scales, in_=grp)
+
+        def quantise_query():
+            quantise(
+                query_grp[:].rearrange("p b i t -> p (b i t)"),
+                query_codes[:].rearrange("p b i -> p (b i)"),
+                query_scales[:].rearrange("p b i -> p (b i)"),
             )
 
-        spread_ps = spread.tile([P, B, 4, P], BF16)
-        for b in range(B):
-            for c in range(4):
-                nc.tensor.transpose(spread_ps[:, b, c, :], not_cb[:, b, c : c + 1].to_broadcast([P, P]), ident_bf16[:])
-        not_cb_all = keep.tile([P, B, K], BF16)
-        nc.vector.tensor_copy(out=not_cb_all[:], in_=spread_ps[:].rearrange("p b c n -> p b (c n)"))
-
-        def context_chunk(b, h):
-            bank = transpose_two_row_tiles(nc, tp, ctx_sb[:].bitcast(F32)[:, b, 2 * h : 2 * h + 2], ident_f32)
-            nc.scalar.copy(out=ctx_grp[:, b, h].bitcast(F32), in_=regrouped(bank))
-            nc.vector.quantize_mx(
-                out=ctx_codes[:, b, h].rearrange("p a n -> p (a n)").bitcast(FP8X4),
-                scales=ctx_scales[:, b, h].rearrange("p a n -> p (a n)"),
-                in_=ctx_grp[:, b, h].rearrange("p a n t -> p (a n t)"),
+        def quantise_w(u):
+            quantise(
+                w_grp[:, u].rearrange("p e m t -> p (e m t)"),
+                w_codes[:, u].rearrange("p e m -> p (e m)"),
+                w_scales[:, u].rearrange("p e m -> p (e m)"),
             )
 
-        context_chunk(0, 0)
-        context_chunk(0, 1)
+        def quantise_context(b, g):
+            quantise(ctx_grp[:, b, g].rearrange("p r e t -> p (r e t)"), ctx_codes[:, b, g, :], ctx_scales[:, b, g, :])
 
-        for b in range(B):
+        def quantise_qt(b):
+            quantise(qt_grp[:, b].rearrange("p i t -> p (i t)"), qt_codes[:, b, :], qt_scales[:, b, :])
+
+        def move_w(u):
+            bank = transpose_two_row_tiles(w_sb[:].bitcast(F32)[:, u])
+            nc.scalar.copy(out=w_grp[:, u].bitcast(F32), in_=bank[:].rearrange("p e u m -> p e m u"))
+
+        def move_context(b, g):
+            bank = transpose_two_row_tiles(ctx_sb[:].bitcast(F32)[:, b, g])
+            nc.scalar.copy(out=ctx_grp[:, b, g].bitcast(F32), in_=bank[:].rearrange("p e u r -> p r e u"))
+
+        def project(b):
             qt_ps = acc.tile([P, PACK, Q], F32, tag="acc")
             for u in range(2):
                 for e in range(2):
@@ -138,20 +126,48 @@ def tile_attention_pa_s_kernel(tc, query, context, query_bit, context_bit, W_in,
                         start=True,
                         stop=True,
                     )
+            return qt_ps
+
+        def add_bias(b, qt_ps):
             nc.vector.tensor_tensor(
                 out=qt_grp[:, b],
                 in0=qt_ps[:].rearrange("p t i -> p i t"),
-                in1=bias_f32[:].unsqueeze(1).to_broadcast([P, Q, PACK]),
+                in1=bias_col[:].unsqueeze(1).to_broadcast([P, Q, PACK]),
                 op=ALU.add,
             )
-            nc.vector.quantize_mx(
-                out=qt_codes[:, b, :].bitcast(FP8X4),
-                scales=qt_scales[:, b, :],
-                in_=qt_grp[:, b].rearrange("p i t -> p (i t)"),
-            )
 
-        context_chunk(1, 0)
-        context_chunk(1, 1)
+        bank = transpose_two_row_tiles(query_sb[:].bitcast(F32))
+        nc.scalar.copy(out=query_grp[:].bitcast(F32), in_=bank[:].rearrange("p b u i -> p b i u"))
+        move_w(0)
+        quantise_query()
+        move_w(1)
+        quantise_w(0)
+        move_context(0, 0)
+        quantise_w(1)
+        move_context(0, 1)
+        quantise_context(0, 0)
+        qt_ps0 = project(0)
+        qt_ps1 = project(1)
+        quantise_context(0, 1)
+        add_bias(0, qt_ps0)
+        move_context(1, 0)
+        add_bias(1, qt_ps1)
+        quantise_qt(0)
+        move_context(1, 1)
+        quantise_qt(1)
+        quantise_context(1, 0)
+
+        not_cb = keep.tile([P, B, 2, 2], BF16)
+        nc.gpsimd.tensor_scalar(out=not_cb[:], in0=cb_col[:], scalar1=-1.0, scalar2=1.0, op0=ALU.mult, op1=ALU.add)
+        neg_qb = keep.tile([P, B], F32)
+        nc.gpsimd.tensor_scalar(out=neg_qb[:], in0=qb_col[:], scalar1=NEG, scalar2=0.0, op0=ALU.mult, op1=ALU.add)
+        spread_ps = spread.tile([P, B, 2, P], F32)
+        for b in range(B):
+            for g in range(2):
+                nc.tensor.transpose(spread_ps[:, b, g, :], not_cb[:].bitcast(F32)[:, b, g, :].to_broadcast([P, P]), ident[:])
+        not_cb_all = keep.tile([P, B, K], BF16)
+        nc.scalar.copy(out=not_cb_all[:].bitcast(F32), in_=spread_ps[:].rearrange("p b g n -> p b (g n)"))
+        quantise_context(1, 1)
 
         masked = keep.tile([P, B, K], F32)
         expd = keep.tile([P, B, K], F32)
@@ -165,8 +181,8 @@ def tile_attention_pa_s_kernel(tc, query, context, query_bit, context_bit, W_in,
                 out=score_ps[:],
                 lhsT=qt_codes[:, b, :].bitcast(FP8X4),
                 lhsT_scale=qt_scales[:, b, :],
-                rhs=ctx_codes[:, b].rearrange("p h a n -> p (h a n)").bitcast(FP8X4),
-                rhs_scale=ctx_scales[:, b].rearrange("p h a n -> p (h a n)"),
+                rhs=ctx_codes[:, b].rearrange("p g n -> p (g n)").bitcast(FP8X4),
+                rhs_scale=ctx_scales[:, b].rearrange("p g n -> p (g n)"),
                 start=True,
                 stop=True,
             )
@@ -189,10 +205,11 @@ def tile_attention_pa_s_kernel(tc, query, context, query_bit, context_bit, W_in,
                 scale=1.0,
                 accum_out=row_sum[:, b : b + 1],
             )
+        for b in range(B):
             nc.vector.reciprocal(inv_sum[:, b : b + 1], row_sum[:, b : b + 1])
             nc.vector.tensor_scalar(
-                out=prob[:, b, :].rearrange("i (p c) -> i p c", c=4),
-                in0=expd[:, b, :].rearrange("i (c p) -> i p c", c=4),
+                out=prob[:, b, :].rearrange("i (p g e) -> i p g e", g=2, e=2),
+                in0=expd[:, b, :].rearrange("i (g p e) -> i p g e", g=2, e=2),
                 scalar1=inv_sum[:, b : b + 1],
                 scalar2=None,
                 op0=ALU.mult,

@@ -17,6 +17,8 @@ Q = 128
 K = 512
 D = 512
 PACK = 4
+WARM_PASSES = 8
+WARM_COLS = 256
 NEG = -10000.0
 
 FLOPS = 2 * B * Q * D * D + 2 * B * Q * K * D
@@ -29,6 +31,7 @@ def tile_attention_pa_s_kernel(tc, query, context, query_bit, context_bit, W_in,
         tp = ctx.enter_context(tc.psum_pool(name="tp", bufs=4))
         spread = ctx.enter_context(tc.psum_pool(name="spread", bufs=1))
         acc = ctx.enter_context(tc.psum_pool(name="acc", bufs=2))
+        idle = ctx.enter_context(tc.psum_pool(name="idle", bufs=1))
         ctx.enter_context(tc.manual_schedule())
 
         query_sb = keep.tile([P, B, D], BF16)
@@ -55,6 +58,23 @@ def tile_attention_pa_s_kernel(tc, query, context, query_bit, context_bit, W_in,
             nc.sync.dma_start(out=qb_col[:], in_=query_bit.rearrange("b i -> i b"))
         nc.sync.dma_start(out=ctx_sb[:, 1, 0], in_=ctx_rows[1, 0])
         nc.sync.dma_start(out=ctx_sb[:, 1, 1], in_=ctx_rows[1, 1])
+
+        zeros = keep.tile([P, WARM_COLS * PACK], BF16, align_bytes=64)
+        zero_codes = keep.tile([P, WARM_COLS], U32, align_bytes=64)
+        zero_scales = keep.tile([P, WARM_COLS], U8, align_bytes=64)
+        nc.vector.memset(zeros[:], 0.0)
+        nc.vector.quantize_mx(out=zero_codes[:].bitcast(FP8X4), scales=zero_scales[:], in_=zeros[:])
+        idle_ps = idle.tile([P, WARM_COLS], F32)
+        for n in range(WARM_PASSES):
+            nc.tensor.matmul_mx(
+                out=idle_ps[:],
+                lhsT=zero_codes[:, 0:P].bitcast(FP8X4),
+                lhsT_scale=zero_scales[:, 0:P],
+                rhs=zero_codes[:].bitcast(FP8X4),
+                rhs_scale=zero_scales[:],
+                start=True,
+                stop=True,
+            )
 
         ident = keep.tile([P, P], F32)
         make_identity(nc, ident[:])

@@ -17,8 +17,6 @@ Q = 128
 K = 512
 D = 512
 PACK = 4
-WARM_PASSES = 8
-WARM_COLS = 256
 NEG = -10000.0
 
 FLOPS = 2 * B * Q * D * D + 2 * B * Q * K * D
@@ -31,7 +29,6 @@ def tile_attention_pa_s_kernel(tc, query, context, query_bit, context_bit, W_in,
         tp = ctx.enter_context(tc.psum_pool(name="tp", bufs=4))
         spread = ctx.enter_context(tc.psum_pool(name="spread", bufs=1))
         acc = ctx.enter_context(tc.psum_pool(name="acc", bufs=2))
-        idle = ctx.enter_context(tc.psum_pool(name="idle", bufs=1))
         ctx.enter_context(tc.manual_schedule())
 
         query_sb = keep.tile([P, B, D], BF16)
@@ -46,41 +43,27 @@ def tile_attention_pa_s_kernel(tc, query, context, query_bit, context_bit, W_in,
             nc.sync.dma_start(out=query_sb[:, b, :], in_=query[b])
         for u in range(2):
             nc.sync.dma_start(out=w_sb[:, u], in_=w_rows[u])
-        nc.sync.dma_start(out=ctx_sb[:, 0, 0], in_=ctx_rows[0, 0])
         nc.sync.dma_start(
             out=bias_col[:].rearrange("p (u e) -> p u e", u=2), in_=b_in.rearrange("(u p e) -> p u e", u=2, e=2)
         )
-        nc.sync.dma_start(out=ctx_sb[:, 0, 1], in_=ctx_rows[0, 1])
         nc.sync.dma_start(
             out=cb_col[:].rearrange("p b g e -> p b (g e)"), in_=context_bit.rearrange("b (p c) -> p b c", c=4)
         )
         with nc.allow_non_contiguous_dma(reason="256 single elements, one to a partition and batch"):
             nc.sync.dma_start(out=qb_col[:], in_=query_bit.rearrange("b i -> i b"))
-        nc.sync.dma_start(out=ctx_sb[:, 1, 0], in_=ctx_rows[1, 0])
-        nc.sync.dma_start(out=ctx_sb[:, 1, 1], in_=ctx_rows[1, 1])
-
-        zeros = keep.tile([P, WARM_COLS * PACK], BF16, align_bytes=64)
-        zero_codes = keep.tile([P, WARM_COLS], U32, align_bytes=64)
-        zero_scales = keep.tile([P, WARM_COLS], U8, align_bytes=64)
-        nc.vector.memset(zeros[:], 0.0)
-        nc.vector.quantize_mx(out=zero_codes[:].bitcast(FP8X4), scales=zero_scales[:], in_=zeros[:])
-        idle_ps = idle.tile([P, WARM_COLS], F32)
-        for n in range(WARM_PASSES):
-            nc.tensor.matmul_mx(
-                out=idle_ps[:],
-                lhsT=zero_codes[:, 0:P].bitcast(FP8X4),
-                lhsT_scale=zero_scales[:, 0:P],
-                rhs=zero_codes[:].bitcast(FP8X4),
-                rhs_scale=zero_scales[:],
-                start=True,
-                stop=True,
-            )
+        for b in range(B):
+            for g in range(2):
+                nc.sync.dma_start(out=ctx_sb[:, b, g], in_=ctx_rows[b, g])
 
         ident = keep.tile([P, P], F32)
         make_identity(nc, ident[:])
         warm = keep.tile([P, 1], F32)
         nc.vector.memset(warm[:], 0.0)
         nc.scalar.activation(out=warm[:], in_=warm[:], func=ACT.Exp)
+        not_cb = keep.tile([P, B, 2, 2], BF16)
+        nc.gpsimd.tensor_scalar(out=not_cb[:], in0=cb_col[:], scalar1=-1.0, scalar2=1.0, op0=ALU.mult, op1=ALU.add)
+        neg_qb = keep.tile([P, B], F32)
+        nc.gpsimd.tensor_scalar(out=neg_qb[:], in0=qb_col[:], scalar1=NEG, scalar2=0.0, op0=ALU.mult, op1=ALU.add)
 
         query_grp = keep.tile([P, B, Q, PACK], BF16, align_bytes=64)
         query_codes = keep.tile([P, B, Q], U32, align_bytes=64)
@@ -122,8 +105,12 @@ def tile_attention_pa_s_kernel(tc, query, context, query_bit, context_bit, W_in,
         def quantise_context(b, g):
             quantise(ctx_grp[:, b, g].rearrange("p r e t -> p (r e t)"), ctx_codes[:, b, g, :], ctx_scales[:, b, g, :])
 
-        def quantise_qt(b):
-            quantise(qt_grp[:, b].rearrange("p i t -> p (i t)"), qt_codes[:, b, :], qt_scales[:, b, :])
+        def quantise_qt():
+            quantise(
+                qt_grp[:].rearrange("p b i t -> p (b i t)"),
+                qt_codes[:].rearrange("p b i -> p (b i)"),
+                qt_scales[:].rearrange("p b i -> p (b i)"),
+            )
 
         def move_w(u):
             bank = transpose_two_row_tiles(w_sb[:].bitcast(F32)[:, u])
@@ -164,29 +151,25 @@ def tile_attention_pa_s_kernel(tc, query, context, query_bit, context_bit, W_in,
         quantise_w(0)
         move_context(0, 0)
         quantise_w(1)
-        move_context(0, 1)
-        quantise_context(0, 0)
         qt_ps0 = project(0)
         qt_ps1 = project(1)
-        quantise_context(0, 1)
-        add_bias(0, qt_ps0)
-        move_context(1, 0)
-        add_bias(1, qt_ps1)
-        quantise_qt(0)
-        move_context(1, 1)
-        quantise_qt(1)
-        quantise_context(1, 0)
 
-        not_cb = keep.tile([P, B, 2, 2], BF16)
-        nc.gpsimd.tensor_scalar(out=not_cb[:], in0=cb_col[:], scalar1=-1.0, scalar2=1.0, op0=ALU.mult, op1=ALU.add)
-        neg_qb = keep.tile([P, B], F32)
-        nc.gpsimd.tensor_scalar(out=neg_qb[:], in0=qb_col[:], scalar1=NEG, scalar2=0.0, op0=ALU.mult, op1=ALU.add)
         spread_ps = spread.tile([P, B, 2, P], F32)
         for b in range(B):
             for g in range(2):
                 nc.tensor.transpose(spread_ps[:, b, g, :], not_cb[:].bitcast(F32)[:, b, g, :].to_broadcast([P, P]), ident[:])
         not_cb_all = keep.tile([P, B, K], BF16)
         nc.scalar.copy(out=not_cb_all[:].bitcast(F32), in_=spread_ps[:].rearrange("p b g n -> p b (g n)"))
+
+        quantise_context(0, 0)
+        add_bias(0, qt_ps0)
+        move_context(0, 1)
+        add_bias(1, qt_ps1)
+        quantise_qt()
+        move_context(1, 0)
+        quantise_context(0, 1)
+        move_context(1, 1)
+        quantise_context(1, 0)
         quantise_context(1, 1)
 
         masked = keep.tile([P, B, K], F32)
@@ -227,11 +210,14 @@ def tile_attention_pa_s_kernel(tc, query, context, query_bit, context_bit, W_in,
             )
         for b in range(B):
             nc.vector.reciprocal(inv_sum[:, b : b + 1], row_sum[:, b : b + 1])
-            nc.vector.tensor_scalar(
-                out=prob[:, b, :].rearrange("i (p g e) -> i p g e", g=2, e=2),
-                in0=expd[:, b, :].rearrange("i (g p e) -> i p g e", g=2, e=2),
-                scalar1=inv_sum[:, b : b + 1],
-                scalar2=None,
-                op0=ALU.mult,
-            )
-            nc.sync.dma_start(out=out[b], in_=prob[:, b, :])
+            for h in range(2):
+                rows = slice(h * (P // 2), (h + 1) * (P // 2))
+                cols = slice(h * (K // 2), (h + 1) * (K // 2))
+                nc.vector.tensor_scalar(
+                    out=prob[:, b, :].rearrange("i (p g e) -> i p g e", g=2, e=2)[:, rows],
+                    in0=expd[:, b, :].rearrange("i (g p e) -> i p g e", g=2, e=2)[:, rows],
+                    scalar1=inv_sum[:, b : b + 1],
+                    scalar2=None,
+                    op0=ALU.mult,
+                )
+                nc.sync.dma_start(out=out[b][:, cols], in_=prob[:, b, cols])

from contextlib import ExitStack

import concourse.mybir as mybir
from concourse.masks import make_identity

F32 = mybir.dt.float32
BF16 = mybir.dt.bfloat16
U32 = mybir.dt.uint32
U8 = mybir.dt.uint8
FP8X4 = mybir.dt.float8_e4m3fn_x4
ALU = mybir.AluOpType
ACT = mybir.ActivationFunctionType

P = 128
B = 2
Q = 128
K = 512
D = 512
PACK = 4
NEG = -10000.0

FLOPS = 2 * B * Q * D * D + 2 * B * Q * K * D


def tile_attention_pa_s_kernel(tc, query, context, query_bit, context_bit, W_in, b_in, out):
    nc = tc.nc
    with ExitStack() as ctx:
        keep = ctx.enter_context(tc.tile_pool(name="keep", bufs=1))
        tp = ctx.enter_context(tc.psum_pool(name="tp", bufs=4))
        spread = ctx.enter_context(tc.psum_pool(name="spread", bufs=1))
        acc = ctx.enter_context(tc.psum_pool(name="acc", bufs=2))
        ctx.enter_context(tc.manual_schedule())

        query_sb = keep.tile([P, B, D], BF16)
        w_sb = keep.tile([P, 2, 2, D], BF16)
        ctx_sb = keep.tile([P, B, 2, 2, D], BF16)
        cb_col = keep.tile([P, B, 2, 2], BF16)
        qb_col = keep.tile([P, B], BF16)
        bias_col = keep.tile([P, PACK], BF16)
        w_rows = W_in.rearrange("(u p e) d -> u p e d", u=2, e=2)
        ctx_rows = context.rearrange("b (p g e) d -> b g p e d", g=2, e=2)
        for b in range(B):
            nc.sync.dma_start(out=query_sb[:, b, :], in_=query[b])
        for u in range(2):
            nc.sync.dma_start(out=w_sb[:, u], in_=w_rows[u])
        nc.sync.dma_start(
            out=bias_col[:].rearrange("p (u e) -> p u e", u=2), in_=b_in.rearrange("(u p e) -> p u e", u=2, e=2)
        )
        nc.sync.dma_start(
            out=cb_col[:].rearrange("p b g e -> p b (g e)"), in_=context_bit.rearrange("b (p c) -> p b c", c=4)
        )
        with nc.allow_non_contiguous_dma(reason="256 single elements, one to a partition and batch"):
            nc.sync.dma_start(out=qb_col[:], in_=query_bit.rearrange("b i -> i b"))
        for b in range(B):
            for g in range(2):
                nc.sync.dma_start(out=ctx_sb[:, b, g], in_=ctx_rows[b, g])

        ident = keep.tile([P, P], F32)
        make_identity(nc, ident[:])
        warm = keep.tile([P, 1], F32)
        nc.vector.memset(warm[:], 0.0)
        nc.scalar.activation(out=warm[:], in_=warm[:], func=ACT.Exp)
        not_cb = keep.tile([P, B, 2, 2], BF16)
        nc.gpsimd.tensor_scalar(out=not_cb[:], in0=cb_col[:], scalar1=-1.0, scalar2=1.0, op0=ALU.mult, op1=ALU.add)
        neg_qb = keep.tile([P, B], F32)
        nc.gpsimd.tensor_scalar(out=neg_qb[:], in0=qb_col[:], scalar1=NEG, scalar2=0.0, op0=ALU.mult, op1=ALU.add)

        query_grp = keep.tile([P, B, Q, PACK], BF16, align_bytes=64)
        query_codes = keep.tile([P, B, Q], U32, align_bytes=64)
        query_scales = keep.tile([P, B, Q], U8, align_bytes=64)
        w_grp = keep.tile([P, 2, 2, P, PACK], BF16, align_bytes=64)
        w_codes = keep.tile([P, 2, 2, P], U32, align_bytes=64)
        w_scales = keep.tile([P, 2, 2, P], U8, align_bytes=64)
        ctx_grp = keep.tile([P, B, 2, P, 2, PACK], BF16, align_bytes=64)
        ctx_codes = keep.tile([P, B, 2, 2 * P], U32, align_bytes=64)
        ctx_scales = keep.tile([P, B, 2, 2 * P], U8, align_bytes=64)
        qt_grp = keep.tile([P, B, Q, PACK], BF16, align_bytes=64)
        qt_codes = keep.tile([P, B, Q], U32, align_bytes=64)
        qt_scales = keep.tile([P, B, Q], U8, align_bytes=64)

        def transpose_two_row_tiles(words):
            bank = tp.tile([P, 2, 2, P], F32)
            for a in range(2):
                for u in range(2):
                    nc.tensor.transpose(bank[:, a, u, :], words[:, a, u * P : (u + 1) * P], ident[:])
            return bank

        def quantise(grp, codes, scales):
            nc.vector.quantize_mx(out=codes.bitcast(FP8X4), scales=scales, in_=grp)

        def quantise_query():
            quantise(
                query_grp[:].rearrange("p b i t -> p (b i t)"),
                query_codes[:].rearrange("p b i -> p (b i)"),
                query_scales[:].rearrange("p b i -> p (b i)"),
            )

        def quantise_w(u):
            quantise(
                w_grp[:, u].rearrange("p e m t -> p (e m t)"),
                w_codes[:, u].rearrange("p e m -> p (e m)"),
                w_scales[:, u].rearrange("p e m -> p (e m)"),
            )

        def quantise_context(b, g):
            quantise(ctx_grp[:, b, g].rearrange("p r e t -> p (r e t)"), ctx_codes[:, b, g, :], ctx_scales[:, b, g, :])

        def quantise_qt():
            quantise(
                qt_grp[:].rearrange("p b i t -> p (b i t)"),
                qt_codes[:].rearrange("p b i -> p (b i)"),
                qt_scales[:].rearrange("p b i -> p (b i)"),
            )

        def move_w(u):
            bank = transpose_two_row_tiles(w_sb[:].bitcast(F32)[:, u])
            nc.scalar.copy(out=w_grp[:, u].bitcast(F32), in_=bank[:].rearrange("p e u m -> p e m u"))

        def move_context(b, g):
            bank = transpose_two_row_tiles(ctx_sb[:].bitcast(F32)[:, b, g])
            nc.scalar.copy(out=ctx_grp[:, b, g].bitcast(F32), in_=bank[:].rearrange("p e u r -> p r e u"))

        def project(b):
            qt_ps = acc.tile([P, PACK, Q], F32, tag="acc")
            for u in range(2):
                for e in range(2):
                    nc.tensor.matmul_mx(
                        out=qt_ps[:, 2 * u + e, :],
                        lhsT=w_codes[:, u, e, :].bitcast(FP8X4),
                        lhsT_scale=w_scales[:, u, e, :],
                        rhs=query_codes[:, b, :].bitcast(FP8X4),
                        rhs_scale=query_scales[:, b, :],
                        start=True,
                        stop=True,
                    )
            return qt_ps

        def add_bias(b, qt_ps):
            nc.vector.tensor_tensor(
                out=qt_grp[:, b],
                in0=qt_ps[:].rearrange("p t i -> p i t"),
                in1=bias_col[:].unsqueeze(1).to_broadcast([P, Q, PACK]),
                op=ALU.add,
            )

        bank = transpose_two_row_tiles(query_sb[:].bitcast(F32))
        nc.scalar.copy(out=query_grp[:].bitcast(F32), in_=bank[:].rearrange("p b u i -> p b i u"))
        move_w(0)
        quantise_query()
        move_w(1)
        quantise_w(0)
        move_context(0, 0)
        quantise_w(1)
        qt_ps0 = project(0)
        qt_ps1 = project(1)

        spread_ps = spread.tile([P, B, 2, P], F32)
        for b in range(B):
            for g in range(2):
                nc.tensor.transpose(spread_ps[:, b, g, :], not_cb[:].bitcast(F32)[:, b, g, :].to_broadcast([P, P]), ident[:])
        not_cb_all = keep.tile([P, B, K], BF16)
        nc.scalar.copy(out=not_cb_all[:].bitcast(F32), in_=spread_ps[:].rearrange("p b g n -> p b (g n)"))

        quantise_context(0, 0)
        add_bias(0, qt_ps0)
        move_context(0, 1)
        add_bias(1, qt_ps1)
        quantise_qt()
        move_context(1, 0)
        quantise_context(0, 1)
        move_context(1, 1)
        quantise_context(1, 0)
        quantise_context(1, 1)

        masked = keep.tile([P, B, K], F32)
        expd = keep.tile([P, B, K], F32)
        prob = keep.tile([P, B, K], F32)
        neg_max = keep.tile([P, B], F32)
        row_sum = keep.tile([P, B], F32)
        inv_sum = keep.tile([P, B], F32)
        for b in range(B):
            score_ps = acc.tile([P, K], F32, tag="acc")
            nc.tensor.matmul_mx(
                out=score_ps[:],
                lhsT=qt_codes[:, b, :].bitcast(FP8X4),
                lhsT_scale=qt_scales[:, b, :],
                rhs=ctx_codes[:, b].rearrange("p g n -> p (g n)").bitcast(FP8X4),
                rhs_scale=ctx_scales[:, b].rearrange("p g n -> p (g n)"),
                start=True,
                stop=True,
            )
            nc.vector.scalar_tensor_tensor(
                out=masked[:, b, :],
                in0=not_cb_all[:, b, :],
                scalar=neg_qb[:, b : b + 1],
                in1=score_ps[:],
                op0=ALU.mult,
                op1=ALU.add,
            )
            nc.vector.tensor_reduce(
                out=neg_max[:, b : b + 1], in_=masked[:, b, :], axis=mybir.AxisListType.X, op=ALU.max, negate=True
            )
            nc.scalar.activation(
                out=expd[:, b, :],
                in_=masked[:, b, :],
                func=ACT.Exp,
                bias=neg_max[:, b : b + 1],
                scale=1.0,
                accum_out=row_sum[:, b : b + 1],
            )
        for b in range(B):
            nc.vector.reciprocal(inv_sum[:, b : b + 1], row_sum[:, b : b + 1])
            for h in range(2):
                rows = slice(h * (P // 2), (h + 1) * (P // 2))
                cols = slice(h * (K // 2), (h + 1) * (K // 2))
                nc.vector.tensor_scalar(
                    out=prob[:, b, :].rearrange("i (p g e) -> i p g e", g=2, e=2)[:, rows],
                    in0=expd[:, b, :].rearrange("i (g p e) -> i p g e", g=2, e=2)[:, rows],
                    scalar1=inv_sum[:, b : b + 1],
                    scalar2=None,
                    op0=ALU.mult,
                )
                nc.sync.dma_start(out=out[b][:, cols], in_=prob[:, b, cols])
